import numpy as np
import ml_dtypes


def mxq(x, axis, fmt="e4m3"):
    dtype, down = {"e4m3": (ml_dtypes.float8_e4m3fn, 7), "e5m2": (ml_dtypes.float8_e5m2, 14)}[fmt]
    v = np.moveaxis(np.asarray(x, np.float32).astype(ml_dtypes.bfloat16).astype(np.float64), axis, -1)
    blocks = v.reshape(v.shape[:-1] + (-1, 32))
    amax = np.abs(blocks).max(-1, keepdims=True)
    byte = np.maximum(np.where(amax > 0, np.frexp(amax)[1] - 1 + 127, 0) - down, 1)
    scale = np.exp2(byte - 127.0)
    codes = (blocks / scale).astype(np.float32).astype(dtype).astype(np.float64)
    return np.moveaxis((codes * scale).reshape(v.shape), -1, axis)


WIDE = False


def mx_kscale(k):
    if not WIDE:
        return np.ones(k)
    levels = np.array([30, -30])
    if k % 512:
        return np.exp2(np.random.permutation(np.resize(levels, k // 32))).repeat(32)
    a = np.empty((k // 512, 16))
    for p in range(k // 512):
        a[p, :8] = np.random.permutation(np.resize(levels, 8))
        for g in range(8):
            far = levels[np.abs(levels - a[p, g]) >= 10]
            a[p, g + 8] = far[np.random.randint(len(far))]
    return np.exp2(a.ravel()).repeat(32)


BF16 = ml_dtypes.bfloat16


def bf(x):
    return np.asarray(x, np.float32).astype(BF16)


def f64(x):
    return np.asarray(x).astype(np.float64)


C_COUNT, NC, ROW, COL = 8, 48, 512, 512


def setup_inputs():
    s = mx_kscale(ROW)
    return {"Pb": bf(np.random.standard_normal((C_COUNT, ROW, ROW)) * 1.25 / np.sqrt(ROW)),
            "Ev": bf(np.random.standard_normal((C_COUNT, ROW, ROW)) * s),
            "W_pie": bf(np.random.standard_normal((C_COUNT, ROW, ROW)) / np.sqrt(ROW) / s[:, None]),
            "feat": bf(np.random.standard_normal((C_COUNT, ROW, COL)))}


def reference(Pb, Ev, W_pie, feat):
    T = mxq(f64(Ev), 2, "e5m2") @ mxq(f64(W_pie), 1, "e4m3")
    d = (f64(Pb) * T.transpose(0, 2, 1)).sum(-1)
    return 0.3 * d[:, :, None] * f64(feat) + f64(feat)

@@ -1,0 +1,157 @@
+from contextlib import ExitStack
+
+import concourse.mybir as mybir
+from concourse.masks import make_identity
+
+C = 8
+R = 512
+FLOPS = 2 * C * R * R * R + 4 * C * R * R
+
+F32 = mybir.dt.float32
+BF16 = mybir.dt.bfloat16
+U32 = mybir.dt.uint32
+U8 = mybir.dt.uint8
+E4M3X4 = mybir.dt.float8_e4m3fn_x4
+E5M2X4 = mybir.dt.float8_e5m2_x4
+MULT = mybir.AluOpType.mult
+COPY = mybir.ActivationFunctionType.Copy
+
+P = 128
+A = 4
+
+
+def tile_generator_pa_kernel(tc, Pb, Ev, W_pie, feat, out):
+    nc = tc.nc
+
+    def rows_of(dram, c):
+        return dram.flatten_outer_dims()[c * R : (c + 1) * R, :].rearrange("(p a) x -> p (a x)", a=A)
+
+    with ExitStack() as ctx:
+        const = ctx.enter_context(tc.tile_pool(name="const", bufs=1))
+        inputs = ctx.enter_context(tc.tile_pool(name="inputs", bufs=C))
+        results = ctx.enter_context(tc.tile_pool(name="results", bufs=6))
+        work = ctx.enter_context(tc.tile_pool(name="work", bufs=2))
+        psum_t = ctx.enter_context(tc.psum_pool(name="psum_t", bufs=2))
+        psum_acc = ctx.enter_context(tc.psum_pool(name="psum_acc", bufs=1))
+
+        ident = const.tile([P, P], F32, name="ident")
+        make_identity(nc, ident[:])
+        warm_in = const.tile([P, 1], F32, name="warm_in")
+        warm_out = const.tile([P, 1], F32, name="warm_out")
+
+        ev_in, w_in, pb_in, feat_in = [], [], [], []
+        evg, wg, ev_codes, ev_scales, w_codes, w_scales = {}, {}, {}, {}, {}, {}
+        xt, acc, d3, gain, res = {}, {}, {}, {}, {}
+
+        def load(c):
+            for dram, keep, tag in ((Ev, ev_in, "ev_in"), (W_pie, w_in, "w_in"), (Pb, pb_in, "pb_in"), (feat, feat_in, "feat_in")):
+                t = inputs.tile([P, A * R], BF16, name=tag)
+                nc.sync.dma_start(out=t[:], in_=rows_of(dram, c))
+                keep.append(t)
+
+        def transposes(c):
+            words = ev_in[c][:].bitcast(F32)
+            for b in range(2):
+                bank = psum_t.tile([P, 512], F32, name="xt%d" % b)
+                for w in range(4):
+                    a, u = 2 * b + w // 2, w % 2
+                    nc.tensor.transpose(bank[:, w * P : (w + 1) * P], words[:, 256 * a + u : 256 * (a + 1) : 2], ident[:])
+                xt[(c, b)] = bank
+
+        def copy_out(c):
+            g = work.tile([P, 4 * R], BF16, name="evg", align_bytes=64)
+            g_words = g[:].bitcast(F32).rearrange("p (r b w) -> p b r w", b=2, w=4)
+            for b in range(2):
+                nc.scalar.copy(out=g_words[:, b], in_=xt[(c, b)][:].rearrange("p (w r) -> p r w", w=4))
+            evg[c] = g
+
+        def interleave_w(c):
+            g = work.tile([P, 4 * R], BF16, name="wg", align_bytes=64)
+            nc.vector.tensor_copy(
+                out=g[:].rearrange("p (a m t) -> p a m t", a=A, t=4),
+                in_=w_in[c][:].rearrange("p (t m a) -> p a m t", t=4, a=A),
+            )
+            wg[c] = g
+
+        def quantize_ev(c):
+            codes = work.tile([P, R], U32, name="ev_codes", align_bytes=64)
+            scales = work.tile([P, R], U8, name="ev_scales", align_bytes=64)
+            nc.vector.quantize_mx(out=codes[:].bitcast(E5M2X4), scales=scales[:], in_=evg[c][:])
+            ev_codes[c], ev_scales[c] = codes, scales
+
+        def quantize_w(c):
+            codes = work.tile([P, R], U32, name="w_codes", align_bytes=64)
+            scales = work.tile([P, R], U8, name="w_scales", align_bytes=64)
+            nc.vector.quantize_mx(out=codes[:].bitcast(E4M3X4), scales=scales[:], in_=wg[c][:])
+            w_codes[c], w_scales[c] = codes, scales
+
+        def multiply(c):
+            for a in range(A):
+                bank = psum_acc.tile([P, R], F32, name="acc%d" % a)
+                cols = slice(a * P, (a + 1) * P)
+                nc.tensor.matmul_mx(
+                    out=bank[:],
+                    lhsT=w_codes[c][:, cols].bitcast(E4M3X4),
+                    lhsT_scale=w_scales[c][:, cols],
+                    rhs=ev_codes[c][:].bitcast(E5M2X4),
+                    rhs_scale=ev_scales[c][:],
+                    start=True,
+                    stop=True,
+                )
+                acc[(c, a)] = bank
+
+        def diagonal(c, a):
+            if a == 0:
+                d3[c] = work.tile([P, A], F32, name="d3")
+            junk = work.tile([P, R], F32, name="junk")
+            nc.vector.scalar_tensor_tensor(
+                out=junk[:],
+                in0=acc[(c, a)][:],
+                scalar=0.3,
+                in1=pb_in[c][:, a * R : (a + 1) * R],
+                op0=MULT,
+                op1=MULT,
+                accum_out=d3[c][:, a : a + 1],
+            )
+
+        def make_gain(c):
+            gain[c] = work.tile([P, A], F32, name="gain")
+            nc.vector.tensor_scalar_add(out=gain[c][:], in0=d3[c][:], scalar1=1.0)
+
+        def scale_and_store(c):
+            o = results.tile([P, A * R], F32, name="res")
+            for a in range(A):
+                cols = slice(a * R, (a + 1) * R)
+                nc.scalar.activation(out=o[:, cols], in_=feat_in[c][:, cols], func=COPY, scale=gain[c][:, a : a + 1])
+            nc.sync.dma_start(out=rows_of(out, c), in_=o[:])
+
+        with tc.manual_schedule():
+            nc.vector.memset(warm_in[:], 0.0)
+            nc.scalar.activation(out=warm_out[:], in_=warm_in[:], func=COPY, scale=1.0)
+            for c in range(C):
+                load(c)
+            transposes(0)
+            copy_out(0)
+            interleave_w(0)
+            transposes(1)
+            copy_out(1)
+            quantize_ev(0)
+            quantize_w(0)
+            for c in range(C):
+                multiply(c)
+                if c + 2 < C:
+                    transposes(c + 2)
+                if c + 1 < C:
+                    interleave_w(c + 1)
+                    quantize_ev(c + 1)
+                diagonal(c, 0)
+                if c + 1 < C:
+                    quantize_w(c + 1)
+                for a in range(1, A):
+                    diagonal(c, a)
+                make_gain(c)
+                if c >= 1:
+                    scale_and_store(c - 1)
+                if c + 2 < C:
+                    copy_out(c + 2)
+            scale_and_store(C - 1)

@@ -18,6 +18,7 @@ COPY = mybir.ActivationFunctionType.Copy
 
 P = 128
 A = 4
+W_VECTOR = 3
 
 
 def tile_generator_pa_kernel(tc, Pb, Ev, W_pie, feat, out):
@@ -31,6 +32,7 @@ def tile_generator_pa_kernel(tc, Pb, Ev, W_pie, feat, out):
         inputs = ctx.enter_context(tc.tile_pool(name="inputs", bufs=C))
         results = ctx.enter_context(tc.tile_pool(name="results", bufs=6))
         work = ctx.enter_context(tc.tile_pool(name="work", bufs=2))
+        ahead = ctx.enter_context(tc.tile_pool(name="ahead", bufs=3))
         psum_t = ctx.enter_context(tc.psum_pool(name="psum_t", bufs=2))
         psum_acc = ctx.enter_context(tc.psum_pool(name="psum_acc", bufs=1))
 
@@ -39,15 +41,26 @@ def tile_generator_pa_kernel(tc, Pb, Ev, W_pie, feat, out):
         warm_in = const.tile([P, 1], F32, name="warm_in")
         warm_out = const.tile([P, 1], F32, name="warm_out")
 
-        ev_in, w_in, pb_in, feat_in = [], [], [], []
+        ev_in, w_in, pb_in, feat_in = {}, {}, {}, {}
         evg, wg, ev_codes, ev_scales, w_codes, w_scales = {}, {}, {}, {}, {}, {}
         xt, acc, d3, gain, res = {}, {}, {}, {}, {}
 
-        def load(c):
-            for dram, keep, tag in ((Ev, ev_in, "ev_in"), (W_pie, w_in, "w_in"), (Pb, pb_in, "pb_in"), (feat, feat_in, "feat_in")):
-                t = inputs.tile([P, A * R], BF16, name=tag)
-                nc.sync.dma_start(out=t[:], in_=rows_of(dram, c))
-                keep.append(t)
+        def load(dram, keep, tag, c):
+            t = inputs.tile([P, A * R], BF16, name=tag)
+            nc.sync.dma_start(out=t[:], in_=rows_of(dram, c))
+            keep[c] = t
+
+        def load_w(c):
+            load(W_pie, w_in, "w_in", c)
+
+        def load_ev(c):
+            load(Ev, ev_in, "ev_in", c)
+
+        def load_pb(c):
+            load(Pb, pb_in, "pb_in", c)
+
+        def load_feat(c):
+            load(feat, feat_in, "feat_in", c)
 
         def transposes(c):
             words = ev_in[c][:].bitcast(F32)
@@ -65,13 +78,17 @@ def tile_generator_pa_kernel(tc, Pb, Ev, W_pie, feat, out):
                 nc.scalar.copy(out=g_words[:, b], in_=xt[(c, b)][:].rearrange("p (w r) -> p r w", w=4))
             evg[c] = g
 
-        def interleave_w(c):
+        def interleave_w_scalar(c):
             g = work.tile([P, 4 * R], BF16, name="wg", align_bytes=64)
-            nc.vector.tensor_copy(
-                out=g[:].rearrange("p (a m t) -> p a m t", a=A, t=4),
-                in_=w_in[c][:].rearrange("p (t m a) -> p a m t", t=4, a=A),
-            )
+            dst = g[:].rearrange("p (a m t) -> p m a t", a=A, t=4)
+            src = w_in[c][:].rearrange("p (t m a) -> p m a t", t=4, a=A)
+            nc.scalar.copy(out=dst[:, :, W_VECTOR:A, :], in_=src[:, :, W_VECTOR:A, :])
             wg[c] = g
+
+        def interleave_w_vector(c):
+            dst = wg[c][:].rearrange("p (a m t) -> p m a t", a=A, t=4)
+            src = w_in[c][:].rearrange("p (t m a) -> p m a t", t=4, a=A)
+            nc.vector.tensor_copy(out=dst[:, :, 0:W_VECTOR, :], in_=src[:, :, 0:W_VECTOR, :])
 
         def quantize_ev(c):
             codes = work.tile([P, R], U32, name="ev_codes", align_bytes=64)
@@ -80,8 +97,8 @@ def tile_generator_pa_kernel(tc, Pb, Ev, W_pie, feat, out):
             ev_codes[c], ev_scales[c] = codes, scales
 
         def quantize_w(c):
-            codes = work.tile([P, R], U32, name="w_codes", align_bytes=64)
-            scales = work.tile([P, R], U8, name="w_scales", align_bytes=64)
+            codes = ahead.tile([P, R], U32, name="w_codes", align_bytes=64)
+            scales = ahead.tile([P, R], U8, name="w_scales", align_bytes=64)
             nc.vector.quantize_mx(out=codes[:].bitcast(E4M3X4), scales=scales[:], in_=wg[c][:])
             w_codes[c], w_scales[c] = codes, scales
 
@@ -99,10 +116,11 @@ def tile_generator_pa_kernel(tc, Pb, Ev, W_pie, feat, out):
                     stop=True,
                 )
                 acc[(c, a)] = bank
+            d3[c] = work.tile([P, A], F32, name="d3")
+            gain[c] = work.tile([P, A], F32, name="gain")
+            res[c] = results.tile([P, A * R], F32, name="res")
 
         def diagonal(c, a):
-            if a == 0:
-                d3[c] = work.tile([P, A], F32, name="d3")
             junk = work.tile([P, R], F32, name="junk")
             nc.vector.scalar_tensor_tensor(
                 out=junk[:],
@@ -114,44 +132,75 @@ def tile_generator_pa_kernel(tc, Pb, Ev, W_pie, feat, out):
                 accum_out=d3[c][:, a : a + 1],
             )
 
-        def make_gain(c):
-            gain[c] = work.tile([P, A], F32, name="gain")
-            nc.vector.tensor_scalar_add(out=gain[c][:], in0=d3[c][:], scalar1=1.0)
+        def make_gain(c, a0, a1):
+            nc.vector.tensor_scalar_add(out=gain[c][:, a0:a1], in0=d3[c][:, a0:a1], scalar1=1.0)
 
-        def scale_and_store(c):
-            o = results.tile([P, A * R], F32, name="res")
-            for a in range(A):
-                cols = slice(a * R, (a + 1) * R)
-                nc.scalar.activation(out=o[:, cols], in_=feat_in[c][:, cols], func=COPY, scale=gain[c][:, a : a + 1])
-            nc.sync.dma_start(out=rows_of(out, c), in_=o[:])
+        def scale(c, a):
+            cols = slice(a * R, (a + 1) * R)
+            nc.scalar.activation(out=res[c][:, cols], in_=feat_in[c][:, cols], func=COPY, scale=gain[c][:, a : a + 1])
+
+        def store(c, a0, a1):
+            nc.sync.dma_start(out=rows_of(out, c)[:, a0 * R : a1 * R], in_=res[c][:, a0 * R : a1 * R])
 
         with tc.manual_schedule():
             nc.vector.memset(warm_in[:], 0.0)
             nc.scalar.activation(out=warm_out[:], in_=warm_in[:], func=COPY, scale=1.0)
-            for c in range(C):
-                load(c)
+            load_w(0)
+            load_ev(0)
+            load_w(1)
+            load_pb(0)
+            load_ev(1)
+            for c in range(2, C):
+                load_w(c)
+                load_pb(c - 1)
+                load_ev(c)
+                load_feat(c - 2)
+            load_pb(C - 1)
+            load_feat(C - 2)
+            load_feat(C - 1)
+
+            interleave_w_scalar(0)
+            interleave_w_vector(0)
             transposes(0)
             copy_out(0)
-            interleave_w(0)
+            quantize_w(0)
+            interleave_w_scalar(1)
+            interleave_w_vector(1)
             transposes(1)
             copy_out(1)
             quantize_ev(0)
-            quantize_w(0)
-            for c in range(C):
+            quantize_w(1)
+            for c in range(C - 1):
                 multiply(c)
                 if c + 2 < C:
                     transposes(c + 2)
-                if c + 1 < C:
-                    interleave_w(c + 1)
-                    quantize_ev(c + 1)
-                diagonal(c, 0)
-                if c + 1 < C:
-                    quantize_w(c + 1)
-                for a in range(1, A):
-                    diagonal(c, a)
-                make_gain(c)
+                    interleave_w_scalar(c + 2)
                 if c >= 1:
-                    scale_and_store(c - 1)
+                    for a in range(A):
+                        scale(c - 1, a)
+                    store(c - 1, 0, A)
+                diagonal(c, 0)
+                if c + 2 < C:
+                    interleave_w_vector(c + 2)
+                diagonal(c, 1)
+                quantize_ev(c + 1)
+                diagonal(c, 2)
+                if c + 2 < C:
+                    quantize_w(c + 2)
+                diagonal(c, 3)
+                make_gain(c, 0, A)
                 if c + 2 < C:
                     copy_out(c + 2)
-            scale_and_store(C - 1)
+
+            c = C - 1
+            multiply(c)
+            for a in range(A):
+                scale(c - 1, a)
+            store(c - 1, 0, A)
+            diagonal(c, 0)
+            for a in range(A):
+                if a + 1 < A:
+                    diagonal(c, a + 1)
+                make_gain(c, a, a + 1)
+                scale(c, a)
+                store(c, a, a + 1)

@@ -24,13 +24,15 @@ W_VECTOR = 3
 def tile_generator_pa_kernel(tc, Pb, Ev, W_pie, feat, out):
     nc = tc.nc
 
-    def rows_of(dram, c):
-        return dram.flatten_outer_dims()[c * R : (c + 1) * R, :].rearrange("(p a) x -> p (a x)", a=A)
+    def rows_of(dram, c, n):
+        return dram.flatten_outer_dims()[c * R : (c + n) * R, :].rearrange("(h p a) x -> p h (a x)", h=n, a=A)
 
     with ExitStack() as ctx:
         const = ctx.enter_context(tc.tile_pool(name="const", bufs=1))
-        inputs = ctx.enter_context(tc.tile_pool(name="inputs", bufs=C))
-        results = ctx.enter_context(tc.tile_pool(name="results", bufs=6))
+        first = ctx.enter_context(tc.tile_pool(name="first", bufs=2))
+        inputs = ctx.enter_context(tc.tile_pool(name="inputs", bufs=C // 2 - 1))
+        feats = ctx.enter_context(tc.tile_pool(name="feats", bufs=C // 2))
+        results = ctx.enter_context(tc.tile_pool(name="results", bufs=3))
         work = ctx.enter_context(tc.tile_pool(name="work", bufs=2))
         ahead = ctx.enter_context(tc.tile_pool(name="ahead", bufs=3))
         psum_t = ctx.enter_context(tc.psum_pool(name="psum_t", bufs=2))
@@ -43,27 +45,28 @@ def tile_generator_pa_kernel(tc, Pb, Ev, W_pie, feat, out):
 
         ev_in, w_in, pb_in, feat_in = {}, {}, {}, {}
         evg, wg, ev_codes, ev_scales, w_codes, w_scales = {}, {}, {}, {}, {}, {}
-        xt, acc, d3, gain, res = {}, {}, {}, {}, {}
+        xt, acc, d3, gain, res, res_pair = {}, {}, {}, {}, {}, {}
 
-        def load(dram, keep, tag, c):
-            t = inputs.tile([P, A * R], BF16, name=tag)
-            nc.sync.dma_start(out=t[:], in_=rows_of(dram, c))
-            keep[c] = t
+        def load(pool, dram, keep, tag, c, n):
+            t = pool.tile([P, n, A * R], BF16, name="%s%d" % (tag, n))
+            nc.sync.dma_start(out=t[:], in_=rows_of(dram, c, n))
+            for h in range(n):
+                keep[c + h] = t[:, h, :]
 
-        def load_w(c):
-            load(W_pie, w_in, "w_in", c)
+        def load_w(c, n):
+            load(first if n == 1 else inputs, W_pie, w_in, "w_in", c, n)
 
-        def load_ev(c):
-            load(Ev, ev_in, "ev_in", c)
+        def load_ev(c, n):
+            load(first if n == 1 else inputs, Ev, ev_in, "ev_in", c, n)
 
-        def load_pb(c):
-            load(Pb, pb_in, "pb_in", c)
+        def load_pb(c, n):
+            load(first if n == 1 else inputs, Pb, pb_in, "pb_in", c, n)
 
-        def load_feat(c):
-            load(feat, feat_in, "feat_in", c)
+        def load_feat(c, n):
+            load(feats, feat, feat_in, "feat_in", c, n)
 
         def transposes(c):
-            words = ev_in[c][:].bitcast(F32)
+            words = ev_in[c].bitcast(F32)
             for b in range(2):
                 bank = psum_t.tile([P, 512], F32, name="xt%d" % b)
                 for w in range(4):
@@ -81,13 +84,13 @@ def tile_generator_pa_kernel(tc, Pb, Ev, W_pie, feat, out):
         def interleave_w_scalar(c):
             g = work.tile([P, 4 * R], BF16, name="wg", align_bytes=64)
             dst = g[:].rearrange("p (a m t) -> p m a t", a=A, t=4)
-            src = w_in[c][:].rearrange("p (t m a) -> p m a t", t=4, a=A)
+            src = w_in[c].rearrange("p (t m a) -> p m a t", t=4, a=A)
             nc.scalar.copy(out=dst[:, :, W_VECTOR:A, :], in_=src[:, :, W_VECTOR:A, :])
             wg[c] = g
 
         def interleave_w_vector(c):
             dst = wg[c][:].rearrange("p (a m t) -> p m a t", a=A, t=4)
-            src = w_in[c][:].rearrange("p (t m a) -> p m a t", t=4, a=A)
+            src = w_in[c].rearrange("p (t m a) -> p m a t", t=4, a=A)
             nc.vector.tensor_copy(out=dst[:, :, 0:W_VECTOR, :], in_=src[:, :, 0:W_VECTOR, :])
 
         def quantize_ev(c):
@@ -118,7 +121,10 @@ def tile_generator_pa_kernel(tc, Pb, Ev, W_pie, feat, out):
                 acc[(c, a)] = bank
             d3[c] = work.tile([P, A], F32, name="d3")
             gain[c] = work.tile([P, A], F32, name="gain")
-            res[c] = results.tile([P, A * R], F32, name="res")
+            if c % 2 == 0:
+                pair = results.tile([P, 2, A * R], F32, name="res")
+                res[c], res[c + 1] = pair[:, 0, :], pair[:, 1, :]
+                res_pair[c] = pair
 
         def diagonal(c, a):
             junk = work.tile([P, R], F32, name="junk")
@@ -140,24 +146,26 @@ def tile_generator_pa_kernel(tc, Pb, Ev, W_pie, feat, out):
             nc.scalar.activation(out=res[c][:, cols], in_=feat_in[c][:, cols], func=COPY, scale=gain[c][:, a : a + 1])
 
         def store(c, a0, a1):
-            nc.sync.dma_start(out=rows_of(out, c)[:, a0 * R : a1 * R], in_=res[c][:, a0 * R : a1 * R])
+            nc.sync.dma_start(out=rows_of(out, c, 1)[:, 0, a0 * R : a1 * R], in_=res[c][:, a0 * R : a1 * R])
+
+        def store_pair(c):
+            nc.sync.dma_start(out=rows_of(out, c, 2), in_=res_pair[c][:])
 
         with tc.manual_schedule():
             nc.vector.memset(warm_in[:], 0.0)
             nc.scalar.activation(out=warm_out[:], in_=warm_in[:], func=COPY, scale=1.0)
-            load_w(0)
-            load_ev(0)
-            load_w(1)
-            load_pb(0)
-            load_ev(1)
-            for c in range(2, C):
-                load_w(c)
-                load_pb(c - 1)
-                load_ev(c)
-                load_feat(c - 2)
-            load_pb(C - 1)
-            load_feat(C - 2)
-            load_feat(C - 1)
+            load_w(0, 1)
+            load_ev(0, 1)
+            load_w(1, 1)
+            load_pb(0, 1)
+            load_ev(1, 1)
+            load_pb(1, 1)
+            for c in range(2, C, 2):
+                load_w(c, 2)
+                load_ev(c, 2)
+                load_pb(c, 2)
+                load_feat(c - 2, 2)
+            load_feat(C - 2, 2)
 
             interleave_w_scalar(0)
             interleave_w_vector(0)
@@ -178,7 +186,8 @@ def tile_generator_pa_kernel(tc, Pb, Ev, W_pie, feat, out):
                 if c >= 1:
                     for a in range(A):
                         scale(c - 1, a)
-                    store(c - 1, 0, A)
+                    if c % 2 == 0:
+                        store_pair(c - 2)
                 diagonal(c, 0)
                 if c + 2 < C:
                     interleave_w_vector(c + 2)

@@ -48,7 +48,7 @@ def tile_generator_pa_kernel(tc, Pb, Ev, W_pie, feat, out):
         xt, acc, d3, gain, res, res_pair = {}, {}, {}, {}, {}, {}
 
         def load(pool, dram, keep, tag, c, n):
-            t = pool.tile([P, n, A * R], BF16, name="%s%d" % (tag, n))
+            t = pool.tile([P, n, A * R], BF16, name="%s%d" % (tag, n), align_bytes=256)
             nc.sync.dma_start(out=t[:], in_=rows_of(dram, c, n))
             for h in range(n):
                 keep[c + h] = t[:, h, :]
@@ -122,7 +122,7 @@ def tile_generator_pa_kernel(tc, Pb, Ev, W_pie, feat, out):
             d3[c] = work.tile([P, A], F32, name="d3")
             gain[c] = work.tile([P, A], F32, name="gain")
             if c % 2 == 0:
-                pair = results.tile([P, 2, A * R], F32, name="res")
+                pair = results.tile([P, 2, A * R], F32, name="res", align_bytes=256)
                 res[c], res[c + 1] = pair[:, 0, :], pair[:, 1, :]
                 res_pair[c] = pair
 

@@ -18,20 +18,29 @@ COPY = mybir.ActivationFunctionType.Copy
 
 P = 128
 A = 4
+S = 8
+HALF = 64
+G = C // 2
 W_VECTOR = 3
+W_ALL_SCALAR = (2, 3)
 
 
 def tile_generator_pa_kernel(tc, Pb, Ev, W_pie, feat, out):
     nc = tc.nc
 
-    def rows_of(dram, c, n):
-        return dram.flatten_outer_dims()[c * R : (c + n) * R, :].rearrange("(h p a) x -> p h (a x)", h=n, a=A)
+    def rows_of(dram, c):
+        return dram.flatten_outer_dims()[c * R : (c + 1) * R, :].rearrange("(p a) x -> p (a x)", a=A)
+
+    def pair_rows(dram, g):
+        return dram.flatten_outer_dims()[2 * g * R : 2 * (g + 1) * R, :].rearrange("(q s) x -> q (s x)", s=S)
 
     with ExitStack() as ctx:
         const = ctx.enter_context(tc.tile_pool(name="const", bufs=1))
-        first = ctx.enter_context(tc.tile_pool(name="first", bufs=2))
-        inputs = ctx.enter_context(tc.tile_pool(name="inputs", bufs=C // 2 - 1))
-        feats = ctx.enter_context(tc.tile_pool(name="feats", bufs=C // 2))
+        w_pool = ctx.enter_context(tc.tile_pool(name="w_pool", bufs=4))
+        pb_pool = ctx.enter_context(tc.tile_pool(name="pb_pool", bufs=C))
+        ev_pool = ctx.enter_context(tc.tile_pool(name="ev_pool", bufs=G))
+        feat_pool = ctx.enter_context(tc.tile_pool(name="feat_pool", bufs=G - 1))
+        singles = ctx.enter_context(tc.tile_pool(name="singles", bufs=2))
         results = ctx.enter_context(tc.tile_pool(name="results", bufs=3))
         work = ctx.enter_context(tc.tile_pool(name="work", bufs=2))
         ahead = ctx.enter_context(tc.tile_pool(name="ahead", bufs=3))
@@ -40,63 +49,74 @@ def tile_generator_pa_kernel(tc, Pb, Ev, W_pie, feat, out):
 
         ident = const.tile([P, P], F32, name="ident")
         make_identity(nc, ident[:])
+        pick = const.tile([P, 2, P], F32, name="pick")
+        for e in range(2):
+            for h in range(2):
+                nc.gpsimd.tensor_copy(out=pick[:, e, h * HALF : (h + 1) * HALF], in_=ident[:, e::2])
         warm_in = const.tile([P, 1], F32, name="warm_in")
         warm_out = const.tile([P, 1], F32, name="warm_out")
 
         ev_in, w_in, pb_in, feat_in = {}, {}, {}, {}
         evg, wg, ev_codes, ev_scales, w_codes, w_scales = {}, {}, {}, {}, {}, {}
-        xt, acc, d3, gain, res, res_pair = {}, {}, {}, {}, {}, {}
+        xt, acc, d3, picked, gain, res = {}, {}, {}, {}, {}, {}
+        feat_single, gain_single, res_single = {}, {}, {}
 
-        def load(pool, dram, keep, tag, c, n):
-            t = pool.tile([P, n, A * R], BF16, name="%s%d" % (tag, n), align_bytes=256)
-            nc.sync.dma_start(out=t[:], in_=rows_of(dram, c, n))
-            for h in range(n):
-                keep[c + h] = t[:, h, :]
+        def load(pool, view, keep, tag, i, width):
+            t = pool.tile([P, width], BF16, name=tag, align_bytes=256)
+            nc.sync.dma_start(out=t[:], in_=view)
+            keep[i] = t
 
-        def load_w(c, n):
-            load(first if n == 1 else inputs, W_pie, w_in, "w_in", c, n)
+        def load_w(c):
+            load(w_pool, rows_of(W_pie, c), w_in, "w_in", c, A * R)
 
-        def load_ev(c, n):
-            load(first if n == 1 else inputs, Ev, ev_in, "ev_in", c, n)
+        def load_pb(c):
+            load(pb_pool, rows_of(Pb, c), pb_in, "pb_in", c, A * R)
 
-        def load_pb(c, n):
-            load(first if n == 1 else inputs, Pb, pb_in, "pb_in", c, n)
+        def load_ev(g):
+            load(ev_pool, pair_rows(Ev, g), ev_in, "ev_in", g, S * R)
 
-        def load_feat(c, n):
-            load(feats, feat, feat_in, "feat_in", c, n)
+        def load_feat(g):
+            load(feat_pool, pair_rows(feat, g), feat_in, "feat_in", g, S * R)
 
-        def transposes(c):
-            words = ev_in[c].bitcast(F32)
-            for b in range(2):
-                bank = psum_t.tile([P, 512], F32, name="xt%d" % b)
-                for w in range(4):
-                    a, u = 2 * b + w // 2, w % 2
-                    nc.tensor.transpose(bank[:, w * P : (w + 1) * P], words[:, 256 * a + u : 256 * (a + 1) : 2], ident[:])
-                xt[(c, b)] = bank
+        def load_feat_single(c):
+            load(singles, rows_of(feat, c), feat_single, "feat_single", c, A * R)
 
-        def copy_out(c):
-            g = work.tile([P, 4 * R], BF16, name="evg", align_bytes=64)
-            g_words = g[:].bitcast(F32).rearrange("p (r b w) -> p b r w", b=2, w=4)
-            for b in range(2):
-                nc.scalar.copy(out=g_words[:, b], in_=xt[(c, b)][:].rearrange("p (w r) -> p r w", w=4))
-            evg[c] = g
+        def transposes(g, b):
+            words = ev_in[g][:].bitcast(F32)
+            bank = psum_t.tile([P, 512], F32, name="xt%d" % (b % 2))
+            for w in range(4):
+                s, u = 2 * b + w // 2, w % 2
+                nc.tensor.transpose(bank[:, w * P : (w + 1) * P], words[:, 256 * s + u : 256 * (s + 1) : 2], ident[:])
+            xt[(g, b)] = bank
+
+        def copy_out(g, b):
+            if b == 0:
+                evg[g] = work.tile([P, 2 * 4 * R], BF16, name="evg", align_bytes=64)
+            g_words = evg[g][:].bitcast(F32).rearrange("p (q b w) -> p b q w", b=4, w=4)
+            nc.scalar.copy(out=g_words[:, b], in_=xt[(g, b)][:].rearrange("p (w q) -> p q w", w=4))
 
         def interleave_w_scalar(c):
             g = work.tile([P, 4 * R], BF16, name="wg", align_bytes=64)
             dst = g[:].rearrange("p (a m t) -> p m a t", a=A, t=4)
-            src = w_in[c].rearrange("p (t m a) -> p m a t", t=4, a=A)
-            nc.scalar.copy(out=dst[:, :, W_VECTOR:A, :], in_=src[:, :, W_VECTOR:A, :])
+            src = w_in[c][:].rearrange("p (t m a) -> p m a t", t=4, a=A)
+            a0 = 0 if c in W_ALL_SCALAR else W_VECTOR
+            nc.scalar.copy(out=dst[:, :, a0:A, :], in_=src[:, :, a0:A, :])
             wg[c] = g
 
         def interleave_w_vector(c):
+            if c in W_ALL_SCALAR:
+                return
             dst = wg[c][:].rearrange("p (a m t) -> p m a t", a=A, t=4)
-            src = w_in[c].rearrange("p (t m a) -> p m a t", t=4, a=A)
+            src = w_in[c][:].rearrange("p (t m a) -> p m a t", t=4, a=A)
             nc.vector.tensor_copy(out=dst[:, :, 0:W_VECTOR, :], in_=src[:, :, 0:W_VECTOR, :])
 
         def quantize_ev(c):
             codes = work.tile([P, R], U32, name="ev_codes", align_bytes=64)
             scales = work.tile([P, R], U8, name="ev_scales", align_bytes=64)
-            nc.vector.quantize_mx(out=codes[:].bitcast(E5M2X4), scales=scales[:], in_=evg[c][:])
+            h = c % 2
+            nc.vector.quantize_mx(
+                out=codes[:].bitcast(E5M2X4), scales=scales[:], in_=evg[c // 2][:, h * 4 * R : (h + 1) * 4 * R]
+            )
             ev_codes[c], ev_scales[c] = codes, scales
 
         def quantize_w(c):
@@ -119,15 +139,12 @@ def tile_generator_pa_kernel(tc, Pb, Ev, W_pie, feat, out):
                     stop=True,
                 )
                 acc[(c, a)] = bank
-            d3[c] = work.tile([P, A], F32, name="d3")
-            gain[c] = work.tile([P, A], F32, name="gain")
             if c % 2 == 0:
-                pair = results.tile([P, 2, A * R], F32, name="res", align_bytes=256)
-                res[c], res[c + 1] = pair[:, 0, :], pair[:, 1, :]
-                res_pair[c] = pair
+                d3[c // 2] = work.tile([P, 2 * A], F32, name="d3")
 
         def diagonal(c, a):
             junk = work.tile([P, R], F32, name="junk")
+            col = (c % 2) * A + a
             nc.vector.scalar_tensor_tensor(
                 out=junk[:],
                 in0=acc[(c, a)][:],
@@ -135,81 +152,147 @@ def tile_generator_pa_kernel(tc, Pb, Ev, W_pie, feat, out):
                 in1=pb_in[c][:, a * R : (a + 1) * R],
                 op0=MULT,
                 op1=MULT,
-                accum_out=d3[c][:, a : a + 1],
+                accum_out=d3[c // 2][:, col : col + 1],
             )
 
-        def make_gain(c, a0, a1):
-            nc.vector.tensor_scalar_add(out=gain[c][:, a0:a1], in0=d3[c][:, a0:a1], scalar1=1.0)
+        def pick_gains(g):
+            bank = psum_t.tile([P, 2 * S], F32, name="xt0")
+            for e in range(2):
+                nc.tensor.matmul(out=bank[:, e * S : (e + 1) * S], lhsT=pick[:, e, :], rhs=d3[g][:], start=True, stop=True)
+            picked[g] = bank
 
-        def scale(c, a):
+        def make_gain(g):
+            t = work.tile([P, S], F32, name="gain")
+            for h in range(2):
+                rows = slice(h * HALF, (h + 1) * HALF)
+                nc.vector.tensor_scalar_add(
+                    out=t[rows, :].rearrange("q (e a) -> q e a", a=A),
+                    in0=picked[g][rows, :].rearrange("q (e h a) -> q e h a", h=2, a=A)[:, :, h, :],
+                    scalar1=1.0,
+                )
+            gain[g] = t
+            res[g] = results.tile([P, S * R], F32, name="res", align_bytes=256)
+
+        def scale(g, s):
+            cols = slice(s * R, (s + 1) * R)
+            nc.scalar.activation(out=res[g][:, cols], in_=feat_in[g][:, cols], func=COPY, scale=gain[g][:, s : s + 1])
+
+        def store(g, s0, s1):
+            nc.sync.dma_start(out=pair_rows(out, g)[:, s0 * R : s1 * R], in_=res[g][:, s0 * R : s1 * R])
+
+        def make_gain_single(c, a0, a1):
+            if a0 == 0:
+                gain_single[c] = work.tile([P, A], F32, name="gain_single")
+                res_single[c] = singles.tile([P, A * R], F32, name="res_single", align_bytes=256)
+            h = c % 2
+            nc.vector.tensor_scalar_add(
+                out=gain_single[c][:, a0:a1], in0=d3[c // 2][:, h * A + a0 : h * A + a1], scalar1=1.0
+            )
+
+        def scale_single(c, a):
             cols = slice(a * R, (a + 1) * R)
-            nc.scalar.activation(out=res[c][:, cols], in_=feat_in[c][:, cols], func=COPY, scale=gain[c][:, a : a + 1])
+            nc.scalar.activation(
+                out=res_single[c][:, cols], in_=feat_single[c][:, cols], func=COPY, scale=gain_single[c][:, a : a + 1]
+            )
 
-        def store(c, a0, a1):
-            nc.sync.dma_start(out=rows_of(out, c, 1)[:, 0, a0 * R : a1 * R], in_=res[c][:, a0 * R : a1 * R])
-
-        def store_pair(c):
-            nc.sync.dma_start(out=rows_of(out, c, 2), in_=res_pair[c][:])
+        def store_single(c):
+            nc.sync.dma_start(out=rows_of(out, c), in_=res_single[c][:])
 
         with tc.manual_schedule():
             nc.vector.memset(warm_in[:], 0.0)
             nc.scalar.activation(out=warm_out[:], in_=warm_in[:], func=COPY, scale=1.0)
-            load_w(0, 1)
-            load_ev(0, 1)
-            load_w(1, 1)
-            load_pb(0, 1)
-            load_ev(1, 1)
-            load_pb(1, 1)
-            for c in range(2, C, 2):
-                load_w(c, 2)
-                load_ev(c, 2)
-                load_pb(c, 2)
-                load_feat(c - 2, 2)
-            load_feat(C - 2, 2)
+            load_w(0)
+            load_ev(0)
+            load_w(1)
+            load_pb(0)
+            load_w(2)
+            load_ev(1)
+            load_pb(1)
+            load_w(3)
+            load_ev(2)
+            load_pb(2)
+            load_w(4)
+            load_feat(0)
+            load_pb(3)
+            load_w(5)
+            load_ev(3)
+            load_pb(4)
+            load_w(6)
+            load_feat(1)
+            load_pb(5)
+            load_w(7)
+            load_pb(6)
+            load_pb(7)
+            load_feat(2)
+            load_feat_single(6)
+            load_feat_single(7)
 
             interleave_w_scalar(0)
             interleave_w_vector(0)
-            transposes(0)
-            copy_out(0)
+            for b in range(4):
+                transposes(0, b)
+            for b in range(4):
+                copy_out(0, b)
             quantize_w(0)
             interleave_w_scalar(1)
             interleave_w_vector(1)
-            transposes(1)
-            copy_out(1)
             quantize_ev(0)
             quantize_w(1)
             for c in range(C - 1):
+                g = c // 2
                 multiply(c)
+                if c % 2 == 0 and c >= 2:
+                    pick_gains(g - 1)
+                if c == 0 or (c % 2 == 1 and g + 2 < G):
+                    for b in range(4):
+                        transposes(g + 1 + c % 2, b)
+
                 if c + 2 < C:
-                    transposes(c + 2)
                     interleave_w_scalar(c + 2)
-                if c >= 1:
-                    for a in range(A):
-                        scale(c - 1, a)
-                    if c % 2 == 0:
-                        store_pair(c - 2)
+                if c % 2 == 0 and c >= 2 and g + 1 < G:
+                    copy_out(g + 1, 2)
+                    copy_out(g + 1, 3)
+
                 diagonal(c, 0)
                 if c + 2 < C:
                     interleave_w_vector(c + 2)
+                if c % 2 == 0 and c >= 2:
+                    make_gain(g - 1)
                 diagonal(c, 1)
-                quantize_ev(c + 1)
                 diagonal(c, 2)
+                quantize_ev(c + 1)
+                diagonal(c, 3)
                 if c + 2 < C:
                     quantize_w(c + 2)
-                diagonal(c, 3)
-                make_gain(c, 0, A)
-                if c + 2 < C:
-                    copy_out(c + 2)
+                if c == C - 2:
+                    make_gain_single(c, 0, A)
+
+                if c >= 2:
+                    for s in range(A):
+                        scale(g - 1, (c % 2) * A + s)
+                    if c % 2 == 1:
+                        store(g - 1, 0, S)
+                    if c == C - 2:
+                        store(g - 1, 0, A)
+                if c == 0:
+                    for b in range(4):
+                        copy_out(1, b)
+                if c % 2 == 1 and g + 2 < G:
+                    copy_out(g + 2, 0)
+                    copy_out(g + 2, 1)
 
             c = C - 1
             multiply(c)
+            for s in range(A, S):
+                scale(G - 2, s)
+            store(G - 2, A, S)
             for a in range(A):
-                scale(c - 1, a)
-            store(c - 1, 0, A)
+                scale_single(c - 1, a)
+            store_single(c - 1)
             diagonal(c, 0)
             for a in range(A):
                 if a + 1 < A:
                     diagonal(c, a + 1)
-                make_gain(c, a, a + 1)
-                scale(c, a)
-                store(c, a, a + 1)
+                make_gain_single(c, a, a + 1)
+                scale_single(c, a)
+            store_single(c)

@@ -63,7 +63,7 @@ def tile_generator_pa_kernel(tc, Pb, Ev, W_pie, feat, out):
 
         def load(pool, view, keep, tag, i, width):
             t = pool.tile([P, width], BF16, name=tag, align_bytes=256)
-            nc.sync.dma_start(out=t[:], in_=view)
+            nc.sync.dma_start(out=t[:].bitcast(F32), in_=view.bitcast(F32))
             keep[i] = t
 
         def load_w(c):

@@ -177,8 +177,8 @@ def tile_generator_pa_kernel(tc, Pb, Ev, W_pie, feat, out):
             cols = slice(s * R, (s + 1) * R)
             nc.scalar.activation(out=res[g][:, cols], in_=feat_in[g][:, cols], func=COPY, scale=gain[g][:, s : s + 1])
 
-        def store(g, s0, s1):
-            nc.sync.dma_start(out=pair_rows(out, g)[:, s0 * R : s1 * R], in_=res[g][:, s0 * R : s1 * R])
+        def store(g, s0, s1, queue):
+            queue.dma_start(out=pair_rows(out, g)[:, s0 * R : s1 * R], in_=res[g][:, s0 * R : s1 * R])
 
         def make_gain_single(c, a0, a1):
             if a0 == 0:
@@ -195,8 +195,8 @@ def tile_generator_pa_kernel(tc, Pb, Ev, W_pie, feat, out):
                 out=res_single[c][:, cols], in_=feat_single[c][:, cols], func=COPY, scale=gain_single[c][:, a : a + 1]
             )
 
-        def store_single(c):
-            nc.sync.dma_start(out=rows_of(out, c), in_=res_single[c][:])
+        def store_single(c, queue):
+            queue.dma_start(out=rows_of(out, c), in_=res_single[c][:])
 
         with tc.manual_schedule():
             nc.vector.memset(warm_in[:], 0.0)
@@ -271,9 +271,9 @@ def tile_generator_pa_kernel(tc, Pb, Ev, W_pie, feat, out):
                     for s in range(A):
                         scale(g - 1, (c % 2) * A + s)
                     if c % 2 == 1:
-                        store(g - 1, 0, S)
+                        store(g - 1, 0, S, nc.sync if g == 1 else nc.gpsimd)
                     if c == C - 2:
-                        store(g - 1, 0, A)
+                        store(g - 1, 0, A, nc.sync)
                 if c == 0:
                     for b in range(4):
                         copy_out(1, b)
@@ -285,14 +285,14 @@ def tile_generator_pa_kernel(tc, Pb, Ev, W_pie, feat, out):
             multiply(c)
             for s in range(A, S):
                 scale(G - 2, s)
-            store(G - 2, A, S)
+            store(G - 2, A, S, nc.gpsimd)
             for a in range(A):
                 scale_single(c - 1, a)
-            store_single(c - 1)
+            store_single(c - 1, nc.sync)
             diagonal(c, 0)
             for a in range(A):
                 if a + 1 < A:
                     diagonal(c, a + 1)
                 make_gain_single(c, a, a + 1)
                 scale_single(c, a)
-            store_single(c)
+            store_single(c, nc.gpsimd)

@@ -271,7 +271,7 @@ def tile_generator_pa_kernel(tc, Pb, Ev, W_pie, feat, out):
                     for s in range(A):
                         scale(g - 1, (c % 2) * A + s)
                     if c % 2 == 1:
-                        store(g - 1, 0, S, nc.sync if g == 1 else nc.gpsimd)
+                        store(g - 1, 0, S, nc.sync if g == 1 else nc.scalar)
                     if c == C - 2:
                         store(g - 1, 0, A, nc.sync)
                 if c == 0:
@@ -285,7 +285,7 @@ def tile_generator_pa_kernel(tc, Pb, Ev, W_pie, feat, out):
             multiply(c)
             for s in range(A, S):
                 scale(G - 2, s)
-            store(G - 2, A, S, nc.gpsimd)
+            store(G - 2, A, S, nc.scalar)
             for a in range(A):
                 scale_single(c - 1, a)
             store_single(c - 1, nc.sync)
@@ -295,4 +295,4 @@ def tile_generator_pa_kernel(tc, Pb, Ev, W_pie, feat, out):
                     diagonal(c, a + 1)
                 make_gain_single(c, a, a + 1)
                 scale_single(c, a)
-            store_single(c, nc.gpsimd)
+            store_single(c, nc.scalar)

from contextlib import ExitStack

import concourse.mybir as mybir
from concourse.masks import make_identity

C = 8
R = 512
FLOPS = 2 * C * R * R * R + 4 * C * R * R

F32 = mybir.dt.float32
BF16 = mybir.dt.bfloat16
U32 = mybir.dt.uint32
U8 = mybir.dt.uint8
E4M3X4 = mybir.dt.float8_e4m3fn_x4
E5M2X4 = mybir.dt.float8_e5m2_x4
MULT = mybir.AluOpType.mult
COPY = mybir.ActivationFunctionType.Copy

P = 128
A = 4
S = 8
HALF = 64
G = C // 2
W_VECTOR = 3
W_ALL_SCALAR = (2, 3)


def tile_generator_pa_kernel(tc, Pb, Ev, W_pie, feat, out):
    nc = tc.nc

    def rows_of(dram, c):
        return dram.flatten_outer_dims()[c * R : (c + 1) * R, :].rearrange("(p a) x -> p (a x)", a=A)

    def pair_rows(dram, g):
        return dram.flatten_outer_dims()[2 * g * R : 2 * (g + 1) * R, :].rearrange("(q s) x -> q (s x)", s=S)

    with ExitStack() as ctx:
        const = ctx.enter_context(tc.tile_pool(name="const", bufs=1))
        w_pool = ctx.enter_context(tc.tile_pool(name="w_pool", bufs=4))
        pb_pool = ctx.enter_context(tc.tile_pool(name="pb_pool", bufs=C))
        ev_pool = ctx.enter_context(tc.tile_pool(name="ev_pool", bufs=G))
        feat_pool = ctx.enter_context(tc.tile_pool(name="feat_pool", bufs=G - 1))
        singles = ctx.enter_context(tc.tile_pool(name="singles", bufs=2))
        results = ctx.enter_context(tc.tile_pool(name="results", bufs=3))
        work = ctx.enter_context(tc.tile_pool(name="work", bufs=2))
        ahead = ctx.enter_context(tc.tile_pool(name="ahead", bufs=3))
        psum_t = ctx.enter_context(tc.psum_pool(name="psum_t", bufs=2))
        psum_acc = ctx.enter_context(tc.psum_pool(name="psum_acc", bufs=1))

        ident = const.tile([P, P], F32, name="ident")
        make_identity(nc, ident[:])
        pick = const.tile([P, 2, P], F32, name="pick")
        for e in range(2):
            for h in range(2):
                nc.gpsimd.tensor_copy(out=pick[:, e, h * HALF : (h + 1) * HALF], in_=ident[:, e::2])
        warm_in = const.tile([P, 1], F32, name="warm_in")
        warm_out = const.tile([P, 1], F32, name="warm_out")

        ev_in, w_in, pb_in, feat_in = {}, {}, {}, {}
        evg, wg, ev_codes, ev_scales, w_codes, w_scales = {}, {}, {}, {}, {}, {}
        xt, acc, d3, picked, gain, res = {}, {}, {}, {}, {}, {}
        feat_single, gain_single, res_single = {}, {}, {}

        def load(pool, view, keep, tag, i, width):
            t = pool.tile([P, width], BF16, name=tag, align_bytes=256)
            nc.sync.dma_start(out=t[:].bitcast(F32), in_=view.bitcast(F32))
            keep[i] = t

        def load_w(c):
            load(w_pool, rows_of(W_pie, c), w_in, "w_in", c, A * R)

        def load_pb(c):
            load(pb_pool, rows_of(Pb, c), pb_in, "pb_in", c, A * R)

        def load_ev(g):
            load(ev_pool, pair_rows(Ev, g), ev_in, "ev_in", g, S * R)

        def load_feat(g):
            load(feat_pool, pair_rows(feat, g), feat_in, "feat_in", g, S * R)

        def load_feat_single(c):
            load(singles, rows_of(feat, c), feat_single, "feat_single", c, A * R)

        def transposes(g, b):
            words = ev_in[g][:].bitcast(F32)
            bank = psum_t.tile([P, 512], F32, name="xt%d" % (b % 2))
            for w in range(4):
                s, u = 2 * b + w // 2, w % 2
                nc.tensor.transpose(bank[:, w * P : (w + 1) * P], words[:, 256 * s + u : 256 * (s + 1) : 2], ident[:])
            xt[(g, b)] = bank

        def copy_out(g, b):
            if b == 0:
                evg[g] = work.tile([P, 2 * 4 * R], BF16, name="evg", align_bytes=64)
            g_words = evg[g][:].bitcast(F32).rearrange("p (q b w) -> p b q w", b=4, w=4)
            nc.scalar.copy(out=g_words[:, b], in_=xt[(g, b)][:].rearrange("p (w q) -> p q w", w=4))

        def interleave_w_scalar(c):
            g = work.tile([P, 4 * R], BF16, name="wg", align_bytes=64)
            dst = g[:].rearrange("p (a m t) -> p m a t", a=A, t=4)
            src = w_in[c][:].rearrange("p (t m a) -> p m a t", t=4, a=A)
            a0 = 0 if c in W_ALL_SCALAR else W_VECTOR
            nc.scalar.copy(out=dst[:, :, a0:A, :], in_=src[:, :, a0:A, :])
            wg[c] = g

        def interleave_w_vector(c):
            if c in W_ALL_SCALAR:
                return
            dst = wg[c][:].rearrange("p (a m t) -> p m a t", a=A, t=4)
            src = w_in[c][:].rearrange("p (t m a) -> p m a t", t=4, a=A)
            nc.vector.tensor_copy(out=dst[:, :, 0:W_VECTOR, :], in_=src[:, :, 0:W_VECTOR, :])

        def quantize_ev(c):
            codes = work.tile([P, R], U32, name="ev_codes", align_bytes=64)
            scales = work.tile([P, R], U8, name="ev_scales", align_bytes=64)
            h = c % 2
            nc.vector.quantize_mx(
                out=codes[:].bitcast(E5M2X4), scales=scales[:], in_=evg[c // 2][:, h * 4 * R : (h + 1) * 4 * R]
            )
            ev_codes[c], ev_scales[c] = codes, scales

        def quantize_w(c):
            codes = ahead.tile([P, R], U32, name="w_codes", align_bytes=64)
            scales = ahead.tile([P, R], U8, name="w_scales", align_bytes=64)
            nc.vector.quantize_mx(out=codes[:].bitcast(E4M3X4), scales=scales[:], in_=wg[c][:])
            w_codes[c], w_scales[c] = codes, scales

        def multiply(c):
            for a in range(A):
                bank = psum_acc.tile([P, R], F32, name="acc%d" % a)
                cols = slice(a * P, (a + 1) * P)
                nc.tensor.matmul_mx(
                    out=bank[:],
                    lhsT=w_codes[c][:, cols].bitcast(E4M3X4),
                    lhsT_scale=w_scales[c][:, cols],
                    rhs=ev_codes[c][:].bitcast(E5M2X4),
                    rhs_scale=ev_scales[c][:],
                    start=True,
                    stop=True,
                )
                acc[(c, a)] = bank
            if c % 2 == 0:
                d3[c // 2] = work.tile([P, 2 * A], F32, name="d3")

        def diagonal(c, a):
            junk = work.tile([P, R], F32, name="junk")
            col = (c % 2) * A + a
            nc.vector.scalar_tensor_tensor(
                out=junk[:],
                in0=acc[(c, a)][:],
                scalar=0.3,
                in1=pb_in[c][:, a * R : (a + 1) * R],
                op0=MULT,
                op1=MULT,
                accum_out=d3[c // 2][:, col : col + 1],
            )

        def pick_gains(g):
            bank = psum_t.tile([P, 2 * S], F32, name="xt0")
            for e in range(2):
                nc.tensor.matmul(out=bank[:, e * S : (e + 1) * S], lhsT=pick[:, e, :], rhs=d3[g][:], start=True, stop=True)
            picked[g] = bank

        def make_gain(g):
            t = work.tile([P, S], F32, name="gain")
            for h in range(2):
                rows = slice(h * HALF, (h + 1) * HALF)
                nc.vector.tensor_scalar_add(
                    out=t[rows, :].rearrange("q (e a) -> q e a", a=A),
                    in0=picked[g][rows, :].rearrange("q (e h a) -> q e h a", h=2, a=A)[:, :, h, :],
                    scalar1=1.0,
                )
            gain[g] = t
            res[g] = results.tile([P, S * R], F32, name="res", align_bytes=256)

        def scale(g, s):
            cols = slice(s * R, (s + 1) * R)
            nc.scalar.activation(out=res[g][:, cols], in_=feat_in[g][:, cols], func=COPY, scale=gain[g][:, s : s + 1])

        def store(g, s0, s1, queue):
            queue.dma_start(out=pair_rows(out, g)[:, s0 * R : s1 * R], in_=res[g][:, s0 * R : s1 * R])

        def make_gain_single(c, a0, a1):
            if a0 == 0:
                gain_single[c] = work.tile([P, A], F32, name="gain_single")
                res_single[c] = singles.tile([P, A * R], F32, name="res_single", align_bytes=256)
            h = c % 2
            nc.vector.tensor_scalar_add(
                out=gain_single[c][:, a0:a1], in0=d3[c // 2][:, h * A + a0 : h * A + a1], scalar1=1.0
            )

        def scale_single(c, a):
            cols = slice(a * R, (a + 1) * R)
            nc.scalar.activation(
                out=res_single[c][:, cols], in_=feat_single[c][:, cols], func=COPY, scale=gain_single[c][:, a : a + 1]
            )

        def store_single(c, queue):
            queue.dma_start(out=rows_of(out, c), in_=res_single[c][:])

        with tc.manual_schedule():
            nc.vector.memset(warm_in[:], 0.0)
            nc.scalar.activation(out=warm_out[:], in_=warm_in[:], func=COPY, scale=1.0)
            load_w(0)
            load_ev(0)
            load_w(1)
            load_pb(0)
            load_w(2)
            load_ev(1)
            load_pb(1)
            load_w(3)
            load_ev(2)
            load_pb(2)
            load_w(4)
            load_feat(0)
            load_pb(3)
            load_w(5)
            load_ev(3)
            load_pb(4)
            load_w(6)
            load_feat(1)
            load_pb(5)
            load_w(7)
            load_pb(6)
            load_pb(7)
            load_feat(2)
            load_feat_single(6)
            load_feat_single(7)

            interleave_w_scalar(0)
            interleave_w_vector(0)
            for b in range(4):
                transposes(0, b)
            for b in range(4):
                copy_out(0, b)
            quantize_w(0)
            interleave_w_scalar(1)
            interleave_w_vector(1)
            quantize_ev(0)
            quantize_w(1)
            for c in range(C - 1):
                g = c // 2
                multiply(c)
                if c % 2 == 0 and c >= 2:
                    pick_gains(g - 1)
                if c == 0 or (c % 2 == 1 and g + 2 < G):
                    for b in range(4):
                        transposes(g + 1 + c % 2, b)

                if c + 2 < C:
                    interleave_w_scalar(c + 2)
                if c % 2 == 0 and c >= 2 and g + 1 < G:
                    copy_out(g + 1, 2)
                    copy_out(g + 1, 3)

                diagonal(c, 0)
                if c + 2 < C:
                    interleave_w_vector(c + 2)
                if c % 2 == 0 and c >= 2:
                    make_gain(g - 1)
                diagonal(c, 1)
                diagonal(c, 2)
                quantize_ev(c + 1)
                diagonal(c, 3)
                if c + 2 < C:
                    quantize_w(c + 2)
                if c == C - 2:
                    make_gain_single(c, 0, A)

                if c >= 2:
                    for s in range(A):
                        scale(g - 1, (c % 2) * A + s)
                    if c % 2 == 1:
                        store(g - 1, 0, S, nc.sync if g == 1 else nc.scalar)
                    if c == C - 2:
                        store(g - 1, 0, A, nc.sync)
                if c == 0:
                    for b in range(4):
                        copy_out(1, b)
                if c % 2 == 1 and g + 2 < G:
                    copy_out(g + 2, 0)
                    copy_out(g + 2, 1)

            c = C - 1
            multiply(c)
            for s in range(A, S):
                scale(G - 2, s)
            store(G - 2, A, S, nc.scalar)
            for a in range(A):
                scale_single(c - 1, a)
            store_single(c - 1, nc.sync)
            diagonal(c, 0)
            for a in range(A):
                if a + 1 < A:
                    diagonal(c, a + 1)
                make_gain_single(c, a, a + 1)
                scale_single(c, a)
            store_single(c, nc.scalar)
